import numpy as np
import ml_dtypes


def mxq(x, axis, fmt="e4m3"):
    dtype, down = {"e4m3": (ml_dtypes.float8_e4m3fn, 7), "e5m2": (ml_dtypes.float8_e5m2, 14)}[fmt]
    v = np.moveaxis(np.asarray(x, np.float32).astype(ml_dtypes.bfloat16).astype(np.float64), axis, -1)
    blocks = v.reshape(v.shape[:-1] + (-1, 32))
    amax = np.abs(blocks).max(-1, keepdims=True)
    byte = np.maximum(np.where(amax > 0, np.frexp(amax)[1] - 1 + 127, 0) - down, 1)
    scale = np.exp2(byte - 127.0)
    codes = (blocks / scale).astype(np.float32).astype(dtype).astype(np.float64)
    return np.moveaxis((codes * scale).reshape(v.shape), -1, axis)


WIDE = False


def mx_kscale(k):
    if not WIDE:
        return np.ones(k)
    levels = np.array([18, -18])
    if k % 512:
        return np.exp2(np.random.permutation(np.resize(levels, k // 32))).repeat(32)
    a = np.empty((k // 512, 16))
    for p in range(k // 512):
        a[p, :8] = np.random.permutation(np.resize(levels, 8))
        for g in range(8):
            far = levels[np.abs(levels - a[p, g]) >= 10]
            a[p, g + 8] = far[np.random.randint(len(far))]
    return np.exp2(a.ravel()).repeat(32)


BF16 = ml_dtypes.bfloat16


def bf(x):
    return np.asarray(x, np.float32).astype(BF16)


def f64(x):
    return np.asarray(x).astype(np.float64)


B, D, H = 512, 2048, 1024


def setup_inputs():
    s = mx_kscale(B)[:, None]
    u = mx_kscale(H)
    x0 = bf(np.random.standard_normal((B, D)))
    xz_o = bf(np.random.standard_normal((B, H)) * 0.7)
    h_prev = bf(np.random.standard_normal((B, H)))
    c = bf(np.random.standard_normal((B, H)) * 0.65)
    w_i0 = bf(np.random.standard_normal((D, H)) * 0.7 / np.sqrt(D))
    w_ho = bf(np.random.standard_normal((H, H)) * 0.7 / np.sqrt(H))
    w_co = bf(np.random.standard_normal((H, H)) * 0.7 / np.sqrt(H))
    w_c = bf(np.random.standard_normal((H, H)) * 0.7 / np.sqrt(H))
    b_o = bf(np.random.standard_normal(H) * 0.3)
    g = bf(4.0 * np.random.standard_normal((B, H)) * np.exp2(np.random.randint(-6, 1, (B, 1))) / s * u)
    o = f64(xz_o) + f64(h_prev) @ f64(w_ho) + f64(c) @ f64(w_co) + f64(b_o)
    return {"x": bf(f64(x0) * s),
            "xz_o": xz_o,
            "h_prev": h_prev,
            "c": c,
            "w_i": bf(f64(w_i0) / u),
            "w_ho": w_ho,
            "w_co": w_co,
            "w_c": w_c,
            "b_o": b_o,
            "o": np.asarray(o, np.float32),
            "grad_out": g}


def reference(x, xz_o, h_prev, c, w_i, w_ho, w_co, w_c, b_o, o, grad_out):
    dz = f64(grad_out) * np.tanh(f64(o))
    dx = mxq(dz, 1, "e5m2") @ mxq(f64(w_i), 1, "e4m3").T
    dw_i = mxq(f64(x), 0, "e4m3").T @ mxq(dz, 0, "e5m2")
    return dx, dw_i

@@ -1,0 +1,281 @@
+from contextlib import ExitStack
+
+import concourse.mybir as mybir
+from concourse.masks import make_identity
+
+B, D, H = 512, 2048, 1024
+
+FLOPS = 2 * (2 * B * D * H)
+BYTES = 2 * B * D + 2 * D * H + 4 * B * H + 2 * B * H + 4 * B * D + 4 * D * H
+
+F32 = mybir.dt.float32
+BF16 = mybir.dt.bfloat16
+U32 = mybir.dt.uint32
+U8 = mybir.dt.uint8
+E4M3 = mybir.dt.float8_e4m3fn_x4
+E5M2 = mybir.dt.float8_e5m2_x4
+
+P = 128
+PACK = 4
+SPAN = P * PACK
+BANKS = 8
+D_CHUNKS = D // SPAN
+H_CHUNKS = H // SPAN
+ALIGN = 64
+
+
+def tile_residuallstmcell_pb_v_kernel(
+    tc, x, xz_o, h_prev, c, w_i, w_ho, w_co, w_c, b_o, o, grad_out, out_0, out_1
+):
+    nc = tc.nc
+    with ExitStack() as ctx:
+        sb = ctx.enter_context(tc.tile_pool(name="sb", bufs=1))
+        ps = ctx.enter_context(tc.psum_pool(name="ps", bufs=1))
+        ctx.enter_context(tc.manual_schedule())
+
+        banks_taken = []
+
+        def next_bank():
+            n = len(banks_taken)
+            banks_taken.append(n)
+            return ps.tile([P, SPAN], F32, name="bank%d" % n, tag="bank%d" % (n % BANKS))
+
+        def copy_on(engine, out, in_):
+            if engine == "scalar":
+                nc.scalar.copy(out=out, in_=in_)
+            else:
+                nc.vector.tensor_copy(out=out, in_=in_)
+
+        def mx_tiles(name, width):
+            codes = sb.tile([P, width], U32, name=name + "_codes", align_bytes=ALIGN)
+            scales = sb.tile([P, width], U8, name=name + "_scales", align_bytes=ALIGN)
+            return codes, scales
+
+        def quantize(operand, fmt, values):
+            codes, scales = operand
+            nc.vector.quantize_mx(out=codes[:].bitcast(fmt), scales=scales[:], in_=values[:])
+
+        o_sb = sb.tile([P, PACK * H], F32, name="o_sb", tag="o_then_dx0", align_bytes=ALIGN)
+        g_sb = sb.tile([P, PACK * H], BF16, name="g_sb", tag="g_sb", align_bytes=ALIGN)
+        x_sb = sb.tile([P, PACK * D], BF16, name="x_sb", align_bytes=ALIGN)
+        w_sb = [
+            sb.tile([P, PACK * H], BF16, name="w_sb%d" % dc, align_bytes=ALIGN) for dc in range(D_CHUNKS)
+        ]
+        o_rows = o.rearrange("(p j) h -> p (j h)", j=PACK)
+        w_rows = w_i.rearrange("(dc p r) h -> dc p (r h)", p=P, r=PACK)
+        nc.sync.dma_start(out=w_sb[0][:, : 2 * H], in_=w_rows[0][:, : 2 * H])
+        nc.sync.dma_start(out=w_sb[0][:, 2 * H :], in_=w_rows[0][:, 2 * H :])
+        nc.sync.dma_start(out=o_sb[:, : 2 * H], in_=o_rows[:, : 2 * H])
+        nc.sync.dma_start(out=g_sb[:], in_=grad_out.rearrange("(p j) h -> p (j h)", j=PACK))
+        nc.sync.dma_start(out=o_sb[:, 2 * H : 3 * H], in_=o_rows[:, 2 * H : 3 * H])
+        nc.sync.dma_start(out=o_sb[:, 3 * H :], in_=o_rows[:, 3 * H :])
+        nc.sync.dma_start(out=x_sb[:], in_=x.rearrange("(p j) d -> p (j d)", j=PACK))
+        nc.sync.dma_start(out=w_sb[1][:], in_=w_rows[1])
+        nc.sync.dma_start(out=w_sb[2][:], in_=w_rows[2])
+        nc.sync.dma_start(out=w_sb[3][:], in_=w_rows[3])
+
+        ident = sb.tile([P, P], F32, name="ident", align_bytes=ALIGN)
+        make_identity(nc, ident[:])
+
+        gate = sb.tile([P, PACK * H], F32, name="gate", tag="gate_then_dx1", align_bytes=ALIGN)
+        dz = sb.tile([P, PACK * H], BF16, name="dz", align_bytes=ALIGN)
+        dz_by_h = [
+            sb.tile([P, 2 * H], BF16, name="dz_by_h%d" % jp, align_bytes=ALIGN) for jp in range(2)
+        ]
+        dz_h_mx = [mx_tiles("dz_h%d" % jp, SPAN) for jp in range(2)]
+        dz_by_b = [
+            sb.tile([P, PACK * SPAN], BF16, name="dz_by_b%d" % hc, align_bytes=ALIGN)
+            for hc in range(H_CHUNKS)
+        ]
+        dz_b_mx = [mx_tiles("dz_b%d" % hc, SPAN) for hc in range(H_CHUNKS)]
+        x_mx = [mx_tiles("x%d" % dc, SPAN) for dc in range(D_CHUNKS)]
+        w_mx = [[mx_tiles("w%d_%d" % (dc, hc), SPAN) for hc in range(H_CHUNKS)] for dc in range(D_CHUNKS)]
+        x_by_b = {}
+        w_by_h = {}
+
+        def tanh_gate(j):
+            cols = slice(j * H, (j + 1) * H)
+            nc.scalar.activation(
+                out=gate[:, cols], in_=o_sb[:, cols], func=mybir.ActivationFunctionType.Tanh
+            )
+
+        def make_dz(j):
+            cols = slice(j * H, (j + 1) * H)
+            nc.vector.tensor_tensor(
+                out=dz[:, cols], in0=g_sb[:, cols], in1=gate[:, cols], op=mybir.AluOpType.mult
+            )
+
+        def transpose_pass(dst, words, first_word):
+            for u in range(2):
+                nc.tensor.transpose(
+                    dst[:, u * P : (u + 1) * P],
+                    words[:, first_word + u : first_word + 2 * P : 2],
+                    ident[:],
+                )
+
+        def turn_dz(j, engine):
+            bank = next_bank()
+            words = dz[:, j * H : (j + 1) * H].bitcast(F32)
+            for hc in range(H_CHUNKS):
+                transpose_pass(bank[:, hc * 2 * P : (hc + 1) * 2 * P], words, hc * 2 * P)
+            dst = dz_by_h[j // 2][:].bitcast(F32)[:, (j % 2) * SPAN : (j % 2 + 1) * SPAN]
+            copy_on(
+                engine,
+                dst.rearrange("p (hc m u) -> p hc m u", hc=H_CHUNKS, u=2),
+                bank[:].rearrange("p (hc u m) -> p hc m u", hc=H_CHUNKS, u=2),
+            )
+
+        def turn_w_bank(dc, hc, rp, engine):
+            if rp == 0:
+                w_by_h[dc, hc] = sb.tile(
+                    [P, PACK * SPAN], BF16, name="w_by_h%d_%d" % (dc, hc), tag="w_by_h", bufs=3, align_bytes=ALIGN
+                )
+            words = w_sb[dc][:].bitcast(F32)
+            bank = next_bank()
+            for rr in range(2):
+                first_word = (2 * rp + rr) * (H // 2) + hc * 2 * P
+                transpose_pass(bank[:, rr * 2 * P : (rr + 1) * 2 * P], words, first_word)
+            dst = w_by_h[dc, hc][:].bitcast(F32)[:, rp * SPAN : (rp + 1) * SPAN]
+            copy_on(
+                engine,
+                dst.rearrange("p (m s) -> p m s", s=4),
+                bank[:].rearrange("p (s m) -> p m s", s=4),
+            )
+
+        def turn_w(dc, hc, engines):
+            for rp in range(2):
+                turn_w_bank(dc, hc, rp, engines[rp])
+
+        def interleave_dz(hc, shares):
+            src = dz[:].rearrange("p (j h) -> p j h", j=PACK)[:, :, hc * SPAN : (hc + 1) * SPAN]
+            for engine, q0, q1 in shares:
+                copy_on(
+                    engine,
+                    dz_by_b[hc][:].rearrange("p (q i j) -> p q j i", i=4, j=PACK)[:, q0:q1],
+                    src.rearrange("p j (q i) -> p q j i", i=4)[:, q0:q1],
+                )
+
+        def interleave_x(dc, shares):
+            grouped = sb.tile(
+                [P, PACK * SPAN], BF16, name="x_by_b%d" % dc, tag="x_by_b", bufs=2, align_bytes=ALIGN
+            )
+            x_by_b[dc] = grouped
+            src = x_sb[:].rearrange("p (j d) -> p j d", j=PACK)[:, :, dc * SPAN : (dc + 1) * SPAN]
+            for engine, m0, m1 in shares:
+                copy_on(
+                    engine,
+                    grouped[:].rearrange("p (r m j) -> p m j r", r=PACK, j=PACK)[:, m0:m1],
+                    src.rearrange("p j (m r) -> p m j r", r=PACK)[:, m0:m1],
+                )
+
+        def product(stationary, s_fmt, s_cols, moving, m_fmt, bank, start, stop):
+            nc.tensor.matmul_mx(
+                out=bank[:],
+                lhsT=stationary[0][:, s_cols].bitcast(s_fmt),
+                lhsT_scale=stationary[1][:, s_cols],
+                rhs=moving[0][:].bitcast(m_fmt),
+                rhs_scale=moving[1][:],
+                start=start,
+                stop=stop,
+            )
+
+        def dx_block(stage, first_col, j, dc, engine):
+            bank = next_bank()
+            for hc in range(H_CHUNKS):
+                first = ((j % 2) * H_CHUNKS + hc) * P
+                product(
+                    dz_h_mx[j // 2], E5M2, slice(first, first + P), w_mx[dc][hc], E4M3, bank,
+                    hc == 0, hc == H_CHUNKS - 1,
+                )
+            copy_on(
+                engine,
+                stage[:, first_col : first_col + SPAN].rearrange("p (m rp rr) -> p m rp rr", rp=2, rr=2),
+                bank[:].rearrange("p (rp m rr) -> p m rp rr", rp=2, rr=2),
+            )
+
+        def dw_block(stage, dc, r, hc, engine):
+            bank = next_bank()
+            product(x_mx[dc], E4M3, slice(r * P, (r + 1) * P), dz_b_mx[hc], E5M2, bank, True, True)
+            first = r * H + hc * SPAN
+            copy_on(engine, stage[:, first : first + SPAN], bank[:])
+
+        dx_rows = out_0.rearrange("(p j) d -> p j d", j=PACK)
+        dw_rows = out_1.rearrange("(dc p r) h -> dc p (r h)", p=P, r=PACK)
+
+        def store_dx(stage, half, jp):
+            nc.sync.dma_start(
+                out=dx_rows[:, 2 * jp : 2 * jp + 2, half * 2 * SPAN : (half + 1) * 2 * SPAN],
+                in_=stage[:, jp * 4 * SPAN : (jp + 1) * 4 * SPAN].rearrange("p (j d) -> p j d", j=2),
+            )
+
+        def store_dw(stage, dc, rp):
+            cols = slice(rp * 2 * H, (rp + 1) * 2 * H)
+            nc.sync.dma_start(out=dw_rows[dc][:, cols], in_=stage[:, cols])
+
+        def store_dx_row(stage, j):
+            nc.sync.dma_start(out=dx_rows[:, j, :], in_=stage[:, (j % 2) * D : (j % 2 + 1) * D])
+
+        S, V = "scalar", "vector"
+
+        def store_dx_cols(stage, stage_cols, js, d0, d1):
+            nc.sync.dma_start(
+                out=dx_rows[:, js, d0:d1], in_=stage[:, stage_cols].rearrange("p (j d) -> p j d", d=d1 - d0)
+            )
+
+        def qw(dc, hc):
+            quantize(w_mx[dc][hc], E4M3, w_by_h[dc, hc])
+
+        for rp in range(2):
+            for hc in range(H_CHUNKS):
+                turn_w_bank(0, hc, rp, V)
+        qw(0, 0)
+        qw(0, 1)
+        tanh_gate(0)
+        tanh_gate(1)
+        make_dz(0)
+        make_dz(1)
+        tanh_gate(2)
+        make_dz(2)
+        tanh_gate(3)
+        make_dz(3)
+        for j in range(4):
+            turn_dz(j, S)
+        quantize(dz_h_mx[0], E5M2, dz_by_h[0])
+        interleave_dz(0, [(V, 0, 128)])
+        quantize(dz_h_mx[1], E5M2, dz_by_h[1])
+        interleave_dz(1, [(S, 0, 128)])
+        quantize(dz_b_mx[0], E5M2, dz_by_b[0])
+        interleave_x(0, [(V, 0, 128)])
+        quantize(dz_b_mx[1], E5M2, dz_by_b[1])
+        quantize(x_mx[0], E4M3, x_by_b[0])
+        dx_first = sb.tile([P, PACK * SPAN], F32, name="dx_first", tag="g_sb", align_bytes=ALIGN)
+        dx_rest = [sb.tile([P, 2 * 3 * SPAN], F32, name="dx0", tag="o_then_dx0", align_bytes=ALIGN), sb.tile([P, 2 * 3 * SPAN], F32, name="dx1", tag="gate_then_dx1", align_bytes=ALIGN)]
+        for j in range(4):
+            dx_block(dx_first, j * SPAN, j, 0, S)
+        store_dx_cols(dx_first, slice(0, PACK * SPAN), slice(0, 4), 0, SPAN)
+        units = (1,3,4,5,6,7)
+        pending = [(dc, hc) for dc in range(1, 4) for hc in range(2)]
+        for dc in range(4):
+            dw_stage = sb.tile([P, PACK * H], F32, name="dw%d" % dc, align_bytes=ALIGN)
+            for rp in range(2):
+                step = 2 * dc + rp
+                for r in (2 * rp, 2 * rp + 1):
+                    for hc in range(H_CHUNKS):
+                        dw_block(dw_stage, dc, r, hc, V if (step < 0 and hc == 1) else S)
+                store_dw(dw_stage, dc, rp)
+                if rp == 0 and dc < 3:
+                    interleave_x(dc + 1, [(V, 0, 128)])
+                unit = None
+                if step in units:
+                    unit = pending.pop(0)
+                    turn_w(unit[0], unit[1], [V, V])
+                if rp == 0 and dc < 3:
+                    quantize(x_mx[dc + 1], E4M3, x_by_b[dc + 1])
+                if unit:
+                    qw(unit[0], unit[1])
+        n = 0
+        for j in range(4):
+            for dc in range(1, 4):
+                dx_block(dx_rest[j // 2], ((j % 2) * 3 + dc - 1) * SPAN, j, dc, S if n % 2 == 0 else V)
+                n = n + 1
+            store_dx_cols(dx_rest[j // 2], slice((j % 2) * 3 * SPAN, (j % 2 + 1) * 3 * SPAN), slice(j, j + 1), SPAN, D)

@@ -66,8 +66,9 @@ def tile_residuallstmcell_pb_v_kernel(
         nc.sync.dma_start(out=w_sb[0][:, : 2 * H], in_=w_rows[0][:, : 2 * H])
         nc.sync.dma_start(out=w_sb[0][:, 2 * H :], in_=w_rows[0][:, 2 * H :])
         nc.sync.dma_start(out=o_sb[:, : 2 * H], in_=o_rows[:, : 2 * H])
-        nc.sync.dma_start(out=g_sb[:], in_=grad_out.rearrange("(p j) h -> p (j h)", j=PACK))
+        nc.sync.dma_start(out=g_sb[:, : 2 * H], in_=grad_out.rearrange("(p j) h -> p (j h)", j=PACK)[:, : 2 * H])
         nc.sync.dma_start(out=o_sb[:, 2 * H : 3 * H], in_=o_rows[:, 2 * H : 3 * H])
+        nc.sync.dma_start(out=g_sb[:, 2 * H :], in_=grad_out.rearrange("(p j) h -> p (j h)", j=PACK)[:, 2 * H :])
         nc.sync.dma_start(out=o_sb[:, 3 * H :], in_=o_rows[:, 3 * H :])
         nc.sync.dma_start(out=x_sb[:], in_=x.rearrange("(p j) d -> p (j d)", j=PACK))
         nc.sync.dma_start(out=w_sb[1][:], in_=w_rows[1])
@@ -93,14 +94,14 @@ def tile_residuallstmcell_pb_v_kernel(
         x_by_b = {}
         w_by_h = {}
 
-        def tanh_gate(j):
-            cols = slice(j * H, (j + 1) * H)
+        def tanh_gate(j, h0=0, h1=H):
+            cols = slice(j * H + h0, j * H + h1)
             nc.scalar.activation(
                 out=gate[:, cols], in_=o_sb[:, cols], func=mybir.ActivationFunctionType.Tanh
             )
 
-        def make_dz(j):
-            cols = slice(j * H, (j + 1) * H)
+        def make_dz(j, h0=0, h1=H):
+            cols = slice(j * H + h0, j * H + h1)
             nc.vector.tensor_tensor(
                 out=dz[:, cols], in0=g_sb[:, cols], in1=gate[:, cols], op=mybir.AluOpType.mult
             )
@@ -225,20 +226,24 @@ def tile_residuallstmcell_pb_v_kernel(
         def qw(dc, hc):
             quantize(w_mx[dc][hc], E4M3, w_by_h[dc, hc])
 
-        for rp in range(2):
-            for hc in range(H_CHUNKS):
-                turn_w_bank(0, hc, rp, V)
+        turn_w_bank(0, 0, 0, V)
+        turn_w_bank(0, 1, 0, V)
+        turn_w_bank(0, 0, 1, V)
+        turn_w_bank(0, 1, 1, V)
         qw(0, 0)
-        qw(0, 1)
         tanh_gate(0)
         tanh_gate(1)
         make_dz(0)
         make_dz(1)
+        qw(0, 1)
         tanh_gate(2)
         make_dz(2)
-        tanh_gate(3)
-        make_dz(3)
-        for j in range(4):
+        turn_dz(0, S)
+        tanh_gate(3, 0, SPAN)
+        make_dz(3, 0, SPAN)
+        tanh_gate(3, SPAN, H)
+        make_dz(3, SPAN, H)
+        for j in range(1, 4):
             turn_dz(j, S)
         quantize(dz_h_mx[0], E5M2, dz_by_h[0])
         interleave_dz(0, [(V, 0, 128)])
@@ -249,30 +254,38 @@ def tile_residuallstmcell_pb_v_kernel(
         quantize(dz_b_mx[1], E5M2, dz_by_b[1])
         quantize(x_mx[0], E4M3, x_by_b[0])
         dx_first = sb.tile([P, PACK * SPAN], F32, name="dx_first", tag="g_sb", align_bytes=ALIGN)
-        dx_rest = [sb.tile([P, 2 * 3 * SPAN], F32, name="dx0", tag="o_then_dx0", align_bytes=ALIGN), sb.tile([P, 2 * 3 * SPAN], F32, name="dx1", tag="gate_then_dx1", align_bytes=ALIGN)]
         for j in range(4):
             dx_block(dx_first, j * SPAN, j, 0, S)
         store_dx_cols(dx_first, slice(0, PACK * SPAN), slice(0, 4), 0, SPAN)
-        units = (1,3,4,5,6,7)
+        dx_rest = [sb.tile([P, 2 * 3 * SPAN], F32, name="dx0", tag="o_then_dx0", align_bytes=ALIGN), sb.tile([P, 2 * 3 * SPAN], F32, name="dx1", tag="gate_then_dx1", align_bytes=ALIGN)]
+        units = [1,0,1,1,0,1,1,1,0]
+        vb = [0,0,0,0,0,0,1,1]
         pending = [(dc, hc) for dc in range(1, 4) for hc in range(2)]
+        def units_at(step):
+            turned = [pending.pop(0) for k in range(units[step])]
+            for unit in turned:
+                turn_w(unit[0], unit[1], [V, V])
+            return turned
         for dc in range(4):
             dw_stage = sb.tile([P, PACK * H], F32, name="dw%d" % dc, align_bytes=ALIGN)
             for rp in range(2):
                 step = 2 * dc + rp
-                for r in (2 * rp, 2 * rp + 1):
-                    for hc in range(H_CHUNKS):
-                        dw_block(dw_stage, dc, r, hc, V if (step < 0 and hc == 1) else S)
-                store_dw(dw_stage, dc, rp)
                 if rp == 0 and dc < 3:
                     interleave_x(dc + 1, [(V, 0, 128)])
-                unit = None
-                if step in units:
-                    unit = pending.pop(0)
-                    turn_w(unit[0], unit[1], [V, V])
+                turned = units_at(step)
                 if rp == 0 and dc < 3:
                     quantize(x_mx[dc + 1], E4M3, x_by_b[dc + 1])
-                if unit:
+                for unit in turned:
                     qw(unit[0], unit[1])
+                n = 0
+                for r in (2 * rp, 2 * rp + 1):
+                    for hc in range(H_CHUNKS):
+                        dw_block(dw_stage, dc, r, hc, V if n >= 4 - vb[step] else S)
+                        n = n + 1
+                store_dw(dw_stage, dc, rp)
+        turned = units_at(8)
+        for unit in turned:
+            qw(unit[0], unit[1])
         n = 0
         for j in range(4):
             for dc in range(1, 4):

@@ -211,15 +211,15 @@ def tile_residuallstmcell_pb_v_kernel(
 
         def store_dw(stage, dc, rp):
             cols = slice(rp * 2 * H, (rp + 1) * 2 * H)
-            nc.sync.dma_start(out=dw_rows[dc][:, cols], in_=stage[:, cols])
+            (nc.sync if rp == 0 else nc.scalar).dma_start(out=dw_rows[dc][:, cols], in_=stage[:, cols])
 
         def store_dx_row(stage, j):
             nc.sync.dma_start(out=dx_rows[:, j, :], in_=stage[:, (j % 2) * D : (j % 2 + 1) * D])
 
         S, V = "scalar", "vector"
 
-        def store_dx_cols(stage, stage_cols, js, d0, d1):
-            nc.sync.dma_start(
+        def store_dx_cols(stage, stage_cols, js, d0, d1, queue=nc.sync):
+            queue.dma_start(
                 out=dx_rows[:, js, d0:d1], in_=stage[:, stage_cols].rearrange("p (j d) -> p j d", d=d1 - d0)
             )
 
@@ -261,6 +261,7 @@ def tile_residuallstmcell_pb_v_kernel(
         units = [1,0,1,1,0,1,1,1,0]
         vb = [0,0,0,0,0,0,1,1]
         pending = [(dc, hc) for dc in range(1, 4) for hc in range(2)]
+        held = []
         def units_at(step):
             turned = [pending.pop(0) for k in range(units[step])]
             for unit in turned:
@@ -282,7 +283,12 @@ def tile_residuallstmcell_pb_v_kernel(
                     for hc in range(H_CHUNKS):
                         dw_block(dw_stage, dc, r, hc, V if n >= 4 - vb[step] else S)
                         n = n + 1
-                store_dw(dw_stage, dc, rp)
+                        if n == 1 and held:
+                            store_dw(*held.pop())
+                if rp == 0:
+                    store_dw(dw_stage, dc, rp)
+                else:
+                    held.append((dw_stage, dc, rp))
         turned = units_at(8)
         for unit in turned:
             qw(unit[0], unit[1])
@@ -291,4 +297,6 @@ def tile_residuallstmcell_pb_v_kernel(
             for dc in range(1, 4):
                 dx_block(dx_rest[j // 2], ((j % 2) * 3 + dc - 1) * SPAN, j, dc, S if n % 2 == 0 else V)
                 n = n + 1
-            store_dx_cols(dx_rest[j // 2], slice((j % 2) * 3 * SPAN, (j % 2 + 1) * 3 * SPAN), slice(j, j + 1), SPAN, D)
+                if n == 1:
+                    store_dw(*held.pop())
+            store_dx_cols(dx_rest[j // 2], slice((j % 2) * 3 * SPAN, (j % 2 + 1) * 3 * SPAN), slice(j, j + 1), SPAN, D, nc.sync if j % 2 == 0 else nc.scalar)

from contextlib import ExitStack

import concourse.mybir as mybir
from concourse.masks import make_identity

B, D, H = 512, 2048, 1024

FLOPS = 2 * (2 * B * D * H)
BYTES = 2 * B * D + 2 * D * H + 4 * B * H + 2 * B * H + 4 * B * D + 4 * D * H

F32 = mybir.dt.float32
BF16 = mybir.dt.bfloat16
U32 = mybir.dt.uint32
U8 = mybir.dt.uint8
E4M3 = mybir.dt.float8_e4m3fn_x4
E5M2 = mybir.dt.float8_e5m2_x4

P = 128
PACK = 4
SPAN = P * PACK
BANKS = 8
D_CHUNKS = D // SPAN
H_CHUNKS = H // SPAN
ALIGN = 64


def tile_residuallstmcell_pb_v_kernel(
    tc, x, xz_o, h_prev, c, w_i, w_ho, w_co, w_c, b_o, o, grad_out, out_0, out_1
):
    nc = tc.nc
    with ExitStack() as ctx:
        sb = ctx.enter_context(tc.tile_pool(name="sb", bufs=1))
        ps = ctx.enter_context(tc.psum_pool(name="ps", bufs=1))
        ctx.enter_context(tc.manual_schedule())

        banks_taken = []

        def next_bank():
            n = len(banks_taken)
            banks_taken.append(n)
            return ps.tile([P, SPAN], F32, name="bank%d" % n, tag="bank%d" % (n % BANKS))

        def copy_on(engine, out, in_):
            if engine == "scalar":
                nc.scalar.copy(out=out, in_=in_)
            else:
                nc.vector.tensor_copy(out=out, in_=in_)

        def mx_tiles(name, width):
            codes = sb.tile([P, width], U32, name=name + "_codes", align_bytes=ALIGN)
            scales = sb.tile([P, width], U8, name=name + "_scales", align_bytes=ALIGN)
            return codes, scales

        def quantize(operand, fmt, values):
            codes, scales = operand
            nc.vector.quantize_mx(out=codes[:].bitcast(fmt), scales=scales[:], in_=values[:])

        o_sb = sb.tile([P, PACK * H], F32, name="o_sb", tag="o_then_dx0", align_bytes=ALIGN)
        g_sb = sb.tile([P, PACK * H], BF16, name="g_sb", tag="g_sb", align_bytes=ALIGN)
        x_sb = sb.tile([P, PACK * D], BF16, name="x_sb", align_bytes=ALIGN)
        w_sb = [
            sb.tile([P, PACK * H], BF16, name="w_sb%d" % dc, align_bytes=ALIGN) for dc in range(D_CHUNKS)
        ]
        o_rows = o.rearrange("(p j) h -> p (j h)", j=PACK)
        w_rows = w_i.rearrange("(dc p r) h -> dc p (r h)", p=P, r=PACK)
        nc.sync.dma_start(out=w_sb[0][:, : 2 * H], in_=w_rows[0][:, : 2 * H])
        nc.sync.dma_start(out=w_sb[0][:, 2 * H :], in_=w_rows[0][:, 2 * H :])
        nc.sync.dma_start(out=o_sb[:, : 2 * H], in_=o_rows[:, : 2 * H])
        nc.sync.dma_start(out=g_sb[:, : 2 * H], in_=grad_out.rearrange("(p j) h -> p (j h)", j=PACK)[:, : 2 * H])
        nc.sync.dma_start(out=o_sb[:, 2 * H : 3 * H], in_=o_rows[:, 2 * H : 3 * H])
        nc.sync.dma_start(out=g_sb[:, 2 * H :], in_=grad_out.rearrange("(p j) h -> p (j h)", j=PACK)[:, 2 * H :])
        nc.sync.dma_start(out=o_sb[:, 3 * H :], in_=o_rows[:, 3 * H :])
        nc.sync.dma_start(out=x_sb[:], in_=x.rearrange("(p j) d -> p (j d)", j=PACK))
        nc.sync.dma_start(out=w_sb[1][:], in_=w_rows[1])
        nc.sync.dma_start(out=w_sb[2][:], in_=w_rows[2])
        nc.sync.dma_start(out=w_sb[3][:], in_=w_rows[3])

        ident = sb.tile([P, P], F32, name="ident", align_bytes=ALIGN)
        make_identity(nc, ident[:])

        gate = sb.tile([P, PACK * H], F32, name="gate", tag="gate_then_dx1", align_bytes=ALIGN)
        dz = sb.tile([P, PACK * H], BF16, name="dz", align_bytes=ALIGN)
        dz_by_h = [
            sb.tile([P, 2 * H], BF16, name="dz_by_h%d" % jp, align_bytes=ALIGN) for jp in range(2)
        ]
        dz_h_mx = [mx_tiles("dz_h%d" % jp, SPAN) for jp in range(2)]
        dz_by_b = [
            sb.tile([P, PACK * SPAN], BF16, name="dz_by_b%d" % hc, align_bytes=ALIGN)
            for hc in range(H_CHUNKS)
        ]
        dz_b_mx = [mx_tiles("dz_b%d" % hc, SPAN) for hc in range(H_CHUNKS)]
        x_mx = [mx_tiles("x%d" % dc, SPAN) for dc in range(D_CHUNKS)]
        w_mx = [[mx_tiles("w%d_%d" % (dc, hc), SPAN) for hc in range(H_CHUNKS)] for dc in range(D_CHUNKS)]
        x_by_b = {}
        w_by_h = {}

        def tanh_gate(j, h0=0, h1=H):
            cols = slice(j * H + h0, j * H + h1)
            nc.scalar.activation(
                out=gate[:, cols], in_=o_sb[:, cols], func=mybir.ActivationFunctionType.Tanh
            )

        def make_dz(j, h0=0, h1=H):
            cols = slice(j * H + h0, j * H + h1)
            nc.vector.tensor_tensor(
                out=dz[:, cols], in0=g_sb[:, cols], in1=gate[:, cols], op=mybir.AluOpType.mult
            )

        def transpose_pass(dst, words, first_word):
            for u in range(2):
                nc.tensor.transpose(
                    dst[:, u * P : (u + 1) * P],
                    words[:, first_word + u : first_word + 2 * P : 2],
                    ident[:],
                )

        def turn_dz(j, engine):
            bank = next_bank()
            words = dz[:, j * H : (j + 1) * H].bitcast(F32)
            for hc in range(H_CHUNKS):
                transpose_pass(bank[:, hc * 2 * P : (hc + 1) * 2 * P], words, hc * 2 * P)
            dst = dz_by_h[j // 2][:].bitcast(F32)[:, (j % 2) * SPAN : (j % 2 + 1) * SPAN]
            copy_on(
                engine,
                dst.rearrange("p (hc m u) -> p hc m u", hc=H_CHUNKS, u=2),
                bank[:].rearrange("p (hc u m) -> p hc m u", hc=H_CHUNKS, u=2),
            )

        def turn_w_bank(dc, hc, rp, engine):
            if rp == 0:
                w_by_h[dc, hc] = sb.tile(
                    [P, PACK * SPAN], BF16, name="w_by_h%d_%d" % (dc, hc), tag="w_by_h", bufs=3, align_bytes=ALIGN
                )
            words = w_sb[dc][:].bitcast(F32)
            bank = next_bank()
            for rr in range(2):
                first_word = (2 * rp + rr) * (H // 2) + hc * 2 * P
                transpose_pass(bank[:, rr * 2 * P : (rr + 1) * 2 * P], words, first_word)
            dst = w_by_h[dc, hc][:].bitcast(F32)[:, rp * SPAN : (rp + 1) * SPAN]
            copy_on(
                engine,
                dst.rearrange("p (m s) -> p m s", s=4),
                bank[:].rearrange("p (s m) -> p m s", s=4),
            )

        def turn_w(dc, hc, engines):
            for rp in range(2):
                turn_w_bank(dc, hc, rp, engines[rp])

        def interleave_dz(hc, shares):
            src = dz[:].rearrange("p (j h) -> p j h", j=PACK)[:, :, hc * SPAN : (hc + 1) * SPAN]
            for engine, q0, q1 in shares:
                copy_on(
                    engine,
                    dz_by_b[hc][:].rearrange("p (q i j) -> p q j i", i=4, j=PACK)[:, q0:q1],
                    src.rearrange("p j (q i) -> p q j i", i=4)[:, q0:q1],
                )

        def interleave_x(dc, shares):
            grouped = sb.tile(
                [P, PACK * SPAN], BF16, name="x_by_b%d" % dc, tag="x_by_b", bufs=2, align_bytes=ALIGN
            )
            x_by_b[dc] = grouped
            src = x_sb[:].rearrange("p (j d) -> p j d", j=PACK)[:, :, dc * SPAN : (dc + 1) * SPAN]
            for engine, m0, m1 in shares:
                copy_on(
                    engine,
                    grouped[:].rearrange("p (r m j) -> p m j r", r=PACK, j=PACK)[:, m0:m1],
                    src.rearrange("p j (m r) -> p m j r", r=PACK)[:, m0:m1],
                )

        def product(stationary, s_fmt, s_cols, moving, m_fmt, bank, start, stop):
            nc.tensor.matmul_mx(
                out=bank[:],
                lhsT=stationary[0][:, s_cols].bitcast(s_fmt),
                lhsT_scale=stationary[1][:, s_cols],
                rhs=moving[0][:].bitcast(m_fmt),
                rhs_scale=moving[1][:],
                start=start,
                stop=stop,
            )

        def dx_block(stage, first_col, j, dc, engine):
            bank = next_bank()
            for hc in range(H_CHUNKS):
                first = ((j % 2) * H_CHUNKS + hc) * P
                product(
                    dz_h_mx[j // 2], E5M2, slice(first, first + P), w_mx[dc][hc], E4M3, bank,
                    hc == 0, hc == H_CHUNKS - 1,
                )
            copy_on(
                engine,
                stage[:, first_col : first_col + SPAN].rearrange("p (m rp rr) -> p m rp rr", rp=2, rr=2),
                bank[:].rearrange("p (rp m rr) -> p m rp rr", rp=2, rr=2),
            )

        def dw_block(stage, dc, r, hc, engine):
            bank = next_bank()
            product(x_mx[dc], E4M3, slice(r * P, (r + 1) * P), dz_b_mx[hc], E5M2, bank, True, True)
            first = r * H + hc * SPAN
            copy_on(engine, stage[:, first : first + SPAN], bank[:])

        dx_rows = out_0.rearrange("(p j) d -> p j d", j=PACK)
        dw_rows = out_1.rearrange("(dc p r) h -> dc p (r h)", p=P, r=PACK)

        def store_dx(stage, half, jp):
            nc.sync.dma_start(
                out=dx_rows[:, 2 * jp : 2 * jp + 2, half * 2 * SPAN : (half + 1) * 2 * SPAN],
                in_=stage[:, jp * 4 * SPAN : (jp + 1) * 4 * SPAN].rearrange("p (j d) -> p j d", j=2),
            )

        def store_dw(stage, dc, rp):
            cols = slice(rp * 2 * H, (rp + 1) * 2 * H)
            (nc.sync if rp == 0 else nc.scalar).dma_start(out=dw_rows[dc][:, cols], in_=stage[:, cols])

        def store_dx_row(stage, j):
            nc.sync.dma_start(out=dx_rows[:, j, :], in_=stage[:, (j % 2) * D : (j % 2 + 1) * D])

        S, V = "scalar", "vector"

        def store_dx_cols(stage, stage_cols, js, d0, d1, queue=nc.sync):
            queue.dma_start(
                out=dx_rows[:, js, d0:d1], in_=stage[:, stage_cols].rearrange("p (j d) -> p j d", d=d1 - d0)
            )

        def qw(dc, hc):
            quantize(w_mx[dc][hc], E4M3, w_by_h[dc, hc])

        turn_w_bank(0, 0, 0, V)
        turn_w_bank(0, 1, 0, V)
        turn_w_bank(0, 0, 1, V)
        turn_w_bank(0, 1, 1, V)
        qw(0, 0)
        tanh_gate(0)
        tanh_gate(1)
        make_dz(0)
        make_dz(1)
        qw(0, 1)
        tanh_gate(2)
        make_dz(2)
        turn_dz(0, S)
        tanh_gate(3, 0, SPAN)
        make_dz(3, 0, SPAN)
        tanh_gate(3, SPAN, H)
        make_dz(3, SPAN, H)
        for j in range(1, 4):
            turn_dz(j, S)
        quantize(dz_h_mx[0], E5M2, dz_by_h[0])
        interleave_dz(0, [(V, 0, 128)])
        quantize(dz_h_mx[1], E5M2, dz_by_h[1])
        interleave_dz(1, [(S, 0, 128)])
        quantize(dz_b_mx[0], E5M2, dz_by_b[0])
        interleave_x(0, [(V, 0, 128)])
        quantize(dz_b_mx[1], E5M2, dz_by_b[1])
        quantize(x_mx[0], E4M3, x_by_b[0])
        dx_first = sb.tile([P, PACK * SPAN], F32, name="dx_first", tag="g_sb", align_bytes=ALIGN)
        for j in range(4):
            dx_block(dx_first, j * SPAN, j, 0, S)
        store_dx_cols(dx_first, slice(0, PACK * SPAN), slice(0, 4), 0, SPAN)
        dx_rest = [sb.tile([P, 2 * 3 * SPAN], F32, name="dx0", tag="o_then_dx0", align_bytes=ALIGN), sb.tile([P, 2 * 3 * SPAN], F32, name="dx1", tag="gate_then_dx1", align_bytes=ALIGN)]
        units = [1,0,1,1,0,1,1,1,0]
        vb = [0,0,0,0,0,0,1,1]
        pending = [(dc, hc) for dc in range(1, 4) for hc in range(2)]
        held = []
        def units_at(step):
            turned = [pending.pop(0) for k in range(units[step])]
            for unit in turned:
                turn_w(unit[0], unit[1], [V, V])
            return turned
        for dc in range(4):
            dw_stage = sb.tile([P, PACK * H], F32, name="dw%d" % dc, align_bytes=ALIGN)
            for rp in range(2):
                step = 2 * dc + rp
                if rp == 0 and dc < 3:
                    interleave_x(dc + 1, [(V, 0, 128)])
                turned = units_at(step)
                if rp == 0 and dc < 3:
                    quantize(x_mx[dc + 1], E4M3, x_by_b[dc + 1])
                for unit in turned:
                    qw(unit[0], unit[1])
                n = 0
                for r in (2 * rp, 2 * rp + 1):
                    for hc in range(H_CHUNKS):
                        dw_block(dw_stage, dc, r, hc, V if n >= 4 - vb[step] else S)
                        n = n + 1
                        if n == 1 and held:
                            store_dw(*held.pop())
                if rp == 0:
                    store_dw(dw_stage, dc, rp)
                else:
                    held.append((dw_stage, dc, rp))
        turned = units_at(8)
        for unit in turned:
            qw(unit[0], unit[1])
        n = 0
        for j in range(4):
            for dc in range(1, 4):
                dx_block(dx_rest[j // 2], ((j % 2) * 3 + dc - 1) * SPAN, j, dc, S if n % 2 == 0 else V)
                n = n + 1
                if n == 1:
                    store_dw(*held.pop())
            store_dx_cols(dx_rest[j // 2], slice((j % 2) * 3 * SPAN, (j % 2 + 1) * 3 * SPAN), slice(j, j + 1), SPAN, D, nc.sync if j % 2 == 0 else nc.scalar)
